import numpy as np
import ml_dtypes


def mxq(x, axis, fmt="e4m3"):
    dtype, down = {"e4m3": (ml_dtypes.float8_e4m3fn, 7), "e5m2": (ml_dtypes.float8_e5m2, 14)}[fmt]
    v = np.moveaxis(np.asarray(x, np.float32).astype(ml_dtypes.bfloat16).astype(np.float64), axis, -1)
    blocks = v.reshape(v.shape[:-1] + (-1, 32))
    amax = np.abs(blocks).max(-1, keepdims=True)
    byte = np.maximum(np.where(amax > 0, np.frexp(amax)[1] - 1 + 127, 0) - down, 1)
    scale = np.exp2(byte - 127.0)
    codes = (blocks / scale).astype(np.float32).astype(dtype).astype(np.float64)
    return np.moveaxis((codes * scale).reshape(v.shape), -1, axis)


WIDE = False


def mx_kscale(k):
    if not WIDE:
        return np.ones(k)
    levels = np.array([18, -18])
    if k % 512:
        return np.exp2(np.random.permutation(np.resize(levels, k // 32))).repeat(32)
    a = np.empty((k // 512, 16))
    for p in range(k // 512):
        a[p, :8] = np.random.permutation(np.resize(levels, 8))
        for g in range(8):
            far = levels[np.abs(levels - a[p, g]) >= 10]
            a[p, g + 8] = far[np.random.randint(len(far))]
    return np.exp2(a.ravel()).repeat(32)


BF16 = ml_dtypes.bfloat16


def bf(x):
    return np.asarray(x, np.float32).astype(BF16)


def f64(x):
    return np.asarray(x).astype(np.float64)


N, NFEAT, NHEADS, NHID = 1024, 512, 4, 128
C = NHEADS * NHID
P = 0.08


def elu(v):
    return np.where(v > 0, v, np.exp(np.minimum(v, 0.0)) - 1.0)


def setup_inputs():
    s = mx_kscale(N)
    u = mx_kscale(N)
    v = mx_kscale(C)
    edges = np.random.random((N, N)) < P
    x0 = bf(np.random.standard_normal((N, NFEAT)))
    adj0 = bf(edges * (0.5 + np.random.random((N, N))))
    W00 = bf(np.random.standard_normal((NHEADS, NFEAT, NHID)) * 1.5 / np.sqrt(NFEAT * P * N))
    g = bf(np.random.standard_normal((N, C)) * np.exp2(np.random.randint(-6, 1, (N, 1))) * 0.5 * u[:, None] * v)
    p = f64(adj0) @ (f64(x0) @ f64(W00).transpose(1, 0, 2).reshape(NFEAT, C))
    return {"x": bf(f64(x0) * s[:, None]),
            "adj": bf(f64(adj0) / u[:, None] / s),
            "W0": bf(f64(W00) / v.reshape(NHEADS, 1, NHID)),
            "p": np.asarray(p, np.float32),
            "grad_out": g}


def reference(x, adj, W0, p, grad_out):
    dz2 = f64(grad_out) * np.exp(np.minimum(f64(p), 0.0))
    dz1 = mxq(f64(adj), 0, "e4m3").T @ mxq(dz2, 0, "e5m2")
    w = f64(W0).transpose(1, 0, 2).reshape(NFEAT, C)
    dx = mxq(dz1, 1, "e5m2") @ mxq(w, 1, "e4m3").T
    dw = mxq(f64(x), 0, "e4m3").T @ mxq(dz1, 0, "e5m2")
    return dx, dw.reshape(NFEAT, NHEADS, NHID).transpose(1, 0, 2)

@@ -1,0 +1,308 @@
+from contextlib import ExitStack
+
+import concourse.mybir as mybir
+from concourse.masks import make_identity
+
+N, NFEAT, NHEADS, NHID = 1024, 512, 4, 128
+C = NHEADS * NHID
+P = 128
+J = 4
+G = 512
+FLOPS = 2 * N * N * C + 2 * 2 * N * NFEAT * C
+BYTES = 2 * (N * NFEAT + N * N + NFEAT * C + N * C) + 4 * N * C + 4 * (N * NFEAT + NFEAT * C)
+
+F32 = mybir.dt.float32
+BF16 = mybir.dt.bfloat16
+U32 = mybir.dt.uint32
+U8 = mybir.dt.uint8
+E4 = mybir.dt.float8_e4m3fn_x4
+E5 = mybir.dt.float8_e5m2_x4
+ACT = mybir.ActivationFunctionType
+ALU = mybir.AluOpType
+
+S_SHARE = {(0, 0): 32, (0, 1): 32, (1, 0): 64, (1, 1): 64}
+
+
+def tile_gat_pa_v_kernel(tc, x, adj, W0, p, grad_out, out_0, out_1):
+    nc = tc.nc
+    with ExitStack() as ctx:
+        sb = ctx.enter_context(tc.tile_pool(name="sb", bufs=1))
+        ps = ctx.enter_context(tc.psum_pool(name="ps", bufs=1))
+
+        def st(shape, dtype, name):
+            return sb.tile(shape, dtype, name=name, tag=name, align_bytes=256)
+
+        def bank(i, shape, name):
+            return ps.tile(shape, F32, name=name, tag="b%d" % i)
+
+        adj_raw = {}
+        for g in range(2):
+            adj_raw[0, g] = st([P, J, G], BF16, "ar0%d" % g)
+        adj_raw1 = st([P, J, N], BF16, "ar1")
+        for g in range(2):
+            adj_raw[1, g] = adj_raw1[:, :, G * g : G * (g + 1)]
+        adj_grp = {(k, g): st([P, G, J], BF16, "ag%d%d" % (k, g)) for k in range(2) for g in range(2)}
+        adj_c = {(k, g): st([P, G], U32, "ac%d%d" % (k, g)) for k in range(2) for g in range(2)}
+        adj_s = {(k, g): st([P, G], U8, "as%d%d" % (k, g)) for k in range(2) for g in range(2)}
+        p_raw = [st([P, J, C], F32, "pr%d" % k) for k in range(2)]
+        e_grp = {(k, h): st([P, C // 2, J], F32, "eg%d%d" % (k, h)) for k in range(2) for h in range(2)}
+        g_raw = [st([P, J, C], BF16, "gr%d" % k) for k in range(2)]
+        dz2 = [st([P, C, J], BF16, "dz%d" % k) for k in range(2)]
+        dz2_c = [st([P, C], U32, "dc%d" % k) for k in range(2)]
+        dz2_s = [st([P, C], U8, "ds%d" % k) for k in range(2)]
+        x_raw = [st([P, J, NFEAT], BF16, "xr%d" % k) for k in range(2)]
+        x_grp = [st([P, NFEAT, J], BF16, "xg%d" % k) for k in range(2)]
+        x_c = [st([P, NFEAT], U32, "xc%d" % k) for k in range(2)]
+        x_s = [st([P, NFEAT], U8, "xs%d" % k) for k in range(2)]
+        w_raw = st([P, 4, NHEADS, NHID], BF16, "wr")
+        w_grp = st([P, NFEAT, J], BF16, "wg")
+        w_c = st([P, NFEAT], U32, "wc")
+        w_s = st([P, NFEAT], U8, "ws")
+        dz1 = [st([P, J, C], BF16, "d1%d" % g) for g in range(2)]
+        nd_grp = [st([P, C, J], BF16, "ng%d" % g) for g in range(2)]
+        nd_c = [st([P, C], U32, "nc%d" % g) for g in range(2)]
+        nd_s = [st([P, C], U8, "ns%d" % g) for g in range(2)]
+        ft_grp = [st([P, G, J], BF16, "fg%d" % g) for g in range(2)]
+        ft_c = [st([P, G], U32, "fc%d" % g) for g in range(2)]
+        ft_s = [st([P, G], U8, "fs%d" % g) for g in range(2)]
+        dx = {(g, t): st([P, NFEAT], F32, "dx%d%d" % (g, t)) for g in range(2) for t in range(J)}
+        dw = [st([P, C], F32, "dw%d" % i) for i in range(4)]
+        ident = st([P, P], F32, "ident")
+        warm = st([P, 1], F32, "warm")
+
+        def load_adj(k, g):
+            nc.sync.dma_start(
+                out=adj_raw[k, g][:],
+                in_=adj[G * k : G * (k + 1), G * g : G * (g + 1)].rearrange("(p j) w -> p j w", j=J),
+            )
+
+        def load_adj1():
+            nc.sync.dma_start(out=adj_raw1[:], in_=adj[G:N, :].rearrange("(p j) w -> p j w", j=J))
+
+        def load_p(k):
+            nc.sync.dma_start(out=p_raw[k][:], in_=p[G * k : G * (k + 1), :].rearrange("(p j) w -> p j w", j=J))
+
+        def load_g(k):
+            nc.sync.dma_start(out=g_raw[k][:], in_=grad_out[G * k : G * (k + 1), :].rearrange("(p j) w -> p j w", j=J))
+
+        def load_x(k):
+            nc.sync.dma_start(out=x_raw[k][:], in_=x[G * k : G * (k + 1), :].rearrange("(p j) w -> p j w", j=J))
+
+        def load_w():
+            for h in range(NHEADS):
+                nc.sync.dma_start(out=w_raw[:, :, h, :], in_=W0[h].rearrange("(b p) f -> p b f", p=P))
+
+        def exp_p(k, h):
+            nc.scalar.activation(
+                out=e_grp[k, h][:].rearrange("p (c i) t -> p c t i", i=4),
+                in_=p_raw[k][:, :, 256 * h : 256 * (h + 1)].rearrange("p t (c i) -> p c t i", i=4),
+                func=ACT.Exp,
+            )
+
+        def mul(k, h):
+            c = slice(256 * h, 256 * (h + 1))
+            nc.vector.scalar_tensor_tensor(
+                out=dz2[k][:, c, :],
+                in0=e_grp[k, h][:],
+                scalar=1.0,
+                in1=g_raw[k][:, :, c].rearrange("p t c -> p c t"),
+                op0=ALU.min,
+                op1=ALU.mult,
+            )
+
+        def il_adj(k, g, engine):
+            cut = P - S_SHARE[k, g]
+            m = slice(0, cut) if engine == "v" else slice(cut, P)
+            if m.start == m.stop:
+                return
+            dst = adj_grp[k, g][:].rearrange("p (t m) j -> p m j t", t=J)[:, m]
+            src = adj_raw[k, g][:].rearrange("p j (m t) -> p m j t", t=J)[:, m]
+            if engine == "v":
+                nc.vector.tensor_copy(out=dst, in_=src)
+            else:
+                nc.scalar.copy(out=dst, in_=src)
+
+        def il(grp, raw, engine, c=slice(0, 512)):
+            dst = grp[:, c, :].rearrange("p (c i) t -> p c t i", i=4)
+            s = raw[:, :, c].rearrange("p t (c i) -> p c t i", i=4)
+            if engine == "v":
+                nc.vector.tensor_copy(out=dst, in_=s)
+            else:
+                nc.scalar.copy(out=dst, in_=s)
+
+        def quant(codes, scales, grp, fmt):
+            nc.vector.quantize_mx(out=codes[:].bitcast(fmt), scales=scales[:], in_=grp[:].rearrange("p c j -> p (c j)"))
+
+        def copy(engine, out, in_):
+            if engine == "v":
+                nc.vector.tensor_copy(out=out, in_=in_)
+            else:
+                nc.scalar.copy(out=out, in_=in_)
+
+        acc = {}
+
+        def mm_dz1(k, g):
+            for t in range(J):
+                if k == 0:
+                    acc[g, t] = bank(4 * g + t, [P, C], "acc%d%d" % (g, t))
+                m = slice(P * t, P * (t + 1))
+                nc.tensor.matmul_mx(
+                    out=acc[g, t][:],
+                    lhsT=adj_c[k, g][:, m].bitcast(E4),
+                    lhsT_scale=adj_s[k, g][:, m],
+                    rhs=dz2_c[k][:].bitcast(E5),
+                    rhs_scale=dz2_s[k][:],
+                    start=(k == 0),
+                    stop=(k == 1),
+                )
+
+        def cast(g, t, engine):
+            copy(engine, dz1[g][:, t, :], acc[g, t][:])
+
+        tr = {}
+
+        def trans(key, b, raw_words, blocks):
+            t_ps = bank(b, [P, 2, 2, P], "tr_%s" % key)
+            tr[key] = t_ps
+            for a, blk in enumerate(blocks):
+                for u in range(2):
+                    nc.tensor.transpose(t_ps[:, a, u, :], raw_words[:, 256 * blk + u : 256 * (blk + 1) : 2], ident[:])
+
+        def tr_out(key, grp, half, engine):
+            words = grp[:].rearrange("p c j -> p (c j)").bitcast(F32)
+            copy(
+                engine,
+                words[:, 512 * half : 512 * (half + 1)].rearrange("p (a r u) -> p a r u", a=2, u=2),
+                tr[key][:].rearrange("p a u r -> p a r u"),
+            )
+
+        def words_of(tile3):
+            return tile3.rearrange("p a b -> p (a b)").bitcast(F32)
+
+        def mm_dx(g, t, b):
+            o = bank(b, [P, NFEAT], "dxp%d%d" % (g, t))
+            acc["dx", g, t] = o
+            m = slice(P * t, P * (t + 1))
+            nc.tensor.matmul_mx(
+                out=o[:],
+                lhsT=ft_c[g][:, m].bitcast(E5),
+                lhsT_scale=ft_s[g][:, m],
+                rhs=w_c[:].bitcast(E4),
+                rhs_scale=w_s[:],
+                start=True,
+                stop=True,
+            )
+
+        def dx_out(g, t, engine):
+            copy(engine, dx[g, t][:], acc["dx", g, t][:])
+            nc.sync.dma_start(
+                out=out_0[G * g : G * (g + 1), :].rearrange("(m t) w -> m t w", t=J)[:, t, :], in_=dx[g, t][:]
+            )
+
+        def mm_dw(k, i, b):
+            if k == 0:
+                acc["dw", i] = bank(b, [P, C], "dwp%d" % i)
+            m = slice(P * i, P * (i + 1))
+            nc.tensor.matmul_mx(
+                out=acc["dw", i][:],
+                lhsT=x_c[k][:, m].bitcast(E4),
+                lhsT_scale=x_s[k][:, m],
+                rhs=nd_c[k][:].bitcast(E5),
+                rhs_scale=nd_s[k][:],
+                start=(k == 0),
+                stop=(k == 1),
+            )
+
+        def dw_out(i, engine):
+            copy(engine, dw[i][:], acc["dw", i][:])
+            nc.sync.dma_start(
+                out=out_1[:, P * i : P * (i + 1), :].rearrange("h i f -> i h f"),
+                in_=dw[i][:].rearrange("p (h f) -> p h f", h=NHEADS),
+            )
+
+        with tc.manual_schedule():
+            nc.vector.memset(warm[:], 0.0)
+            nc.scalar.activation(out=warm[:], in_=warm[:], func=ACT.Exp)
+            make_identity(nc, ident[:])
+
+            load_adj(0, 0)
+            load_p(0)
+            load_adj(0, 1)
+            load_g(0)
+            load_p(1)
+            load_g(1)
+            load_adj1()
+            load_w()
+            load_x(0)
+            load_x(1)
+
+            il_adj(0, 0, "s")
+            il_adj(0, 0, "v")
+            quant(adj_c[0, 0], adj_s[0, 0], adj_grp[0, 0], E4)
+            exp_p(0, 0)
+            exp_p(0, 1)
+            il_adj(0, 1, "s")
+            il_adj(0, 1, "v")
+            mul(0, 0)
+            quant(adj_c[0, 1], adj_s[0, 1], adj_grp[0, 1], E4)
+            mul(0, 1)
+            exp_p(1, 0)
+            exp_p(1, 1)
+            quant(dz2_c[0], dz2_s[0], dz2[0], E5)
+            mm_dz1(0, 0)
+            mm_dz1(0, 1)
+            mul(1, 0)
+            mul(1, 1)
+            il_adj(1, 0, "s")
+            il_adj(1, 0, "v")
+            il_adj(1, 1, "s")
+            quant(dz2_c[1], dz2_s[1], dz2[1], E5)
+            quant(adj_c[1, 0], adj_s[1, 0], adj_grp[1, 0], E4)
+            mm_dz1(1, 0)
+            il_adj(1, 1, "v")
+            quant(adj_c[1, 1], adj_s[1, 1], adj_grp[1, 1], E4)
+            mm_dz1(1, 1)
+
+            w_words = w_raw[:].rearrange("p b h f -> p (b h f)").bitcast(F32)
+            d1w = [words_of(dz1[g][:]) for g in range(2)]
+            for t in range(J):
+                cast(0, t, "s")
+            trans("f00", 0, d1w[0], (0, 1))
+            trans("f01", 1, d1w[0], (2, 3))
+            trans("w0", 2, w_words, (0, 1))
+            trans("w1", 3, w_words, (2, 3))
+            for t in range(J):
+                cast(1, t, "v" if t else "v")
+            tr_out("f00", ft_grp[0], 0, "s")
+            tr_out("f01", ft_grp[0], 1, "s")
+            tr_out("w0", w_grp, 0, "s")
+            tr_out("w1", w_grp, 1, "s")
+            trans("f10", 4, d1w[1], (0, 1))
+            trans("f11", 5, d1w[1], (2, 3))
+            il(nd_grp[0], dz1[0], "v")
+            quant(ft_c[0], ft_s[0], ft_grp[0], E5)
+            quant(w_c, w_s, w_grp, E4)
+            tr_out("f10", ft_grp[1], 0, "s")
+            tr_out("f11", ft_grp[1], 1, "s")
+            for t in range(J):
+                mm_dx(0, t, (6, 7, 0, 1)[t])
+            il(nd_grp[1], dz1[1], "v")
+            quant(ft_c[1], ft_s[1], ft_grp[1], E5)
+            for t in range(J):
+                dx_out(0, t, "s")
+            for t in range(J):
+                mm_dx(1, t, (6, 7, 0, 1)[t])
+            quant(nd_c[0], nd_s[0], nd_grp[0], E5)
+            il(x_grp[0], x_raw[0], "v")
+            quant(nd_c[1], nd_s[1], nd_grp[1], E5)
+            quant(x_c[0], x_s[0], x_grp[0], E4)
+            for i in range(4):
+                mm_dw(0, i, 2 + i)
+            for i in range(4):
+                dx_out(1, i, "s")
+            il(x_grp[1], x_raw[1], "v")
+            quant(x_c[1], x_s[1], x_grp[1], E4)
+            for i in range(4):
+                mm_dw(1, i, 2 + i)
+            for i in range(4):
+                dw_out(i, "v" if i % 2 else "s")

@@ -20,9 +20,6 @@ E5 = mybir.dt.float8_e5m2_x4
 ACT = mybir.ActivationFunctionType
 ALU = mybir.AluOpType
 
-S_SHARE = {(0, 0): 32, (0, 1): 32, (1, 0): 64, (1, 1): 64}
-
-
 def tile_gat_pa_v_kernel(tc, x, adj, W0, p, grad_out, out_0, out_1):
     nc = tc.nc
     with ExitStack() as ctx:
@@ -35,12 +32,7 @@ def tile_gat_pa_v_kernel(tc, x, adj, W0, p, grad_out, out_0, out_1):
         def bank(i, shape, name):
             return ps.tile(shape, F32, name=name, tag="b%d" % i)
 
-        adj_raw = {}
-        for g in range(2):
-            adj_raw[0, g] = st([P, J, G], BF16, "ar0%d" % g)
-        adj_raw1 = st([P, J, N], BF16, "ar1")
-        for g in range(2):
-            adj_raw[1, g] = adj_raw1[:, :, G * g : G * (g + 1)]
+        adj_raw = {(k, g): st([P, J, G], BF16, "ar%d%d" % (k, g)) for k in range(2) for g in range(2)}
         adj_grp = {(k, g): st([P, G, J], BF16, "ag%d%d" % (k, g)) for k in range(2) for g in range(2)}
         adj_c = {(k, g): st([P, G], U32, "ac%d%d" % (k, g)) for k in range(2) for g in range(2)}
         adj_s = {(k, g): st([P, G], U8, "as%d%d" % (k, g)) for k in range(2) for g in range(2)}
@@ -76,9 +68,6 @@ def tile_gat_pa_v_kernel(tc, x, adj, W0, p, grad_out, out_0, out_1):
                 in_=adj[G * k : G * (k + 1), G * g : G * (g + 1)].rearrange("(p j) w -> p j w", j=J),
             )
 
-        def load_adj1():
-            nc.sync.dma_start(out=adj_raw1[:], in_=adj[G:N, :].rearrange("(p j) w -> p j w", j=J))
-
         def load_p(k):
             nc.sync.dma_start(out=p_raw[k][:], in_=p[G * k : G * (k + 1), :].rearrange("(p j) w -> p j w", j=J))
 
@@ -110,41 +99,31 @@ def tile_gat_pa_v_kernel(tc, x, adj, W0, p, grad_out, out_0, out_1):
                 op1=ALU.mult,
             )
 
-        def il_adj(k, g, engine):
-            cut = P - S_SHARE[k, g]
-            m = slice(0, cut) if engine == "v" else slice(cut, P)
-            if m.start == m.stop:
-                return
-            dst = adj_grp[k, g][:].rearrange("p (t m) j -> p m j t", t=J)[:, m]
-            src = adj_raw[k, g][:].rearrange("p j (m t) -> p m j t", t=J)[:, m]
-            if engine == "v":
-                nc.vector.tensor_copy(out=dst, in_=src)
-            else:
-                nc.scalar.copy(out=dst, in_=src)
-
-        def il(grp, raw, engine, c=slice(0, 512)):
-            dst = grp[:, c, :].rearrange("p (c i) t -> p c t i", i=4)
-            s = raw[:, :, c].rearrange("p t (c i) -> p c t i", i=4)
-            if engine == "v":
-                nc.vector.tensor_copy(out=dst, in_=s)
-            else:
-                nc.scalar.copy(out=dst, in_=s)
-
-        def quant(codes, scales, grp, fmt):
-            nc.vector.quantize_mx(out=codes[:].bitcast(fmt), scales=scales[:], in_=grp[:].rearrange("p c j -> p (c j)"))
-
         def copy(engine, out, in_):
             if engine == "v":
                 nc.vector.tensor_copy(out=out, in_=in_)
             else:
                 nc.scalar.copy(out=out, in_=in_)
 
+        def il_adj(k, g, engine, m):
+            dst = adj_grp[k, g][:].rearrange("p (t m) j -> p m j t", t=J)[:, m]
+            src = adj_raw[k, g][:].rearrange("p j (m t) -> p m j t", t=J)[:, m]
+            copy(engine, dst, src)
+
+        def il(grp, raw, engine, c=slice(0, 512)):
+            dst = grp[:, c, :].rearrange("p (c i) t -> p c t i", i=4)
+            s = raw[:, :, c].rearrange("p t (c i) -> p c t i", i=4)
+            copy(engine, dst, s)
+
+        def quant(codes, scales, grp, fmt):
+            nc.vector.quantize_mx(out=codes[:].bitcast(fmt), scales=scales[:], in_=grp[:].rearrange("p c j -> p (c j)"))
+
         acc = {}
 
-        def mm_dz1(k, g):
+        def mm_dz1(k, g, banks=None):
             for t in range(J):
                 if k == 0:
-                    acc[g, t] = bank(4 * g + t, [P, C], "acc%d%d" % (g, t))
+                    acc[g, t] = bank(banks[t], [P, C], "acc%d%d" % (g, t))
                 m = slice(P * t, P * (t + 1))
                 nc.tensor.matmul_mx(
                     out=acc[g, t][:],
@@ -220,89 +199,113 @@ def tile_gat_pa_v_kernel(tc, x, adj, W0, p, grad_out, out_0, out_1):
                 in_=dw[i][:].rearrange("p (h f) -> p h f", h=NHEADS),
             )
 
+        w_words = w_raw[:].rearrange("p b h f -> p (b h f)").bitcast(F32)
         with tc.manual_schedule():
             nc.vector.memset(warm[:], 0.0)
             nc.scalar.activation(out=warm[:], in_=warm[:], func=ACT.Exp)
             make_identity(nc, ident[:])
 
-            load_adj(0, 0)
             load_p(0)
-            load_adj(0, 1)
             load_g(0)
             load_p(1)
             load_g(1)
-            load_adj1()
-            load_w()
+            load_adj(0, 1)
+            load_adj(0, 0)
             load_x(0)
+            load_adj(1, 0)
+            load_adj(1, 1)
             load_x(1)
+            load_w()
 
-            il_adj(0, 0, "s")
-            il_adj(0, 0, "v")
-            quant(adj_c[0, 0], adj_s[0, 0], adj_grp[0, 0], E4)
             exp_p(0, 0)
             exp_p(0, 1)
-            il_adj(0, 1, "s")
-            il_adj(0, 1, "v")
             mul(0, 0)
-            quant(adj_c[0, 1], adj_s[0, 1], adj_grp[0, 1], E4)
             mul(0, 1)
-            exp_p(1, 0)
             exp_p(1, 1)
             quant(dz2_c[0], dz2_s[0], dz2[0], E5)
-            mm_dz1(0, 0)
-            mm_dz1(0, 1)
-            mul(1, 0)
+            exp_p(1, 0)
             mul(1, 1)
-            il_adj(1, 0, "s")
-            il_adj(1, 0, "v")
-            il_adj(1, 1, "s")
+            il_adj(0, 1, "s", slice(32, 96))
+            il_adj(0, 1, "v", slice(0, 32))
+            il_adj(0, 1, "v", slice(96, 128))
+            mul(1, 0)
+            il_adj(0, 0, "s", slice(32, 96))
+            il_adj(0, 0, "v", slice(96, 128))
+            il_adj(0, 0, "v", slice(0, 32))
+            quant(adj_c[0, 1], adj_s[0, 1], adj_grp[0, 1], E4)
+            il(x_grp[0], x_raw[0], "s", slice(256, 512))
+            quant(adj_c[0, 0], adj_s[0, 0], adj_grp[0, 0], E4)
+            mm_dz1(0, 1, (0, 1, 2, 3))
             quant(dz2_c[1], dz2_s[1], dz2[1], E5)
+            il_adj(1, 0, "s", slice(0, 32))
+            il_adj(1, 0, "v", slice(32, 64))
+            mm_dz1(0, 0, (4, 5, 6, 7))
+            il_adj(1, 0, "s", slice(64, 96))
+            il_adj(1, 0, "v", slice(96, 128))
+            il(x_grp[0], x_raw[0], "v", slice(0, 256))
+            il_adj(1, 1, "s", slice(0, 64))
             quant(adj_c[1, 0], adj_s[1, 0], adj_grp[1, 0], E4)
+            il(x_grp[1], x_raw[1], "v", slice(256, 512))
+            il_adj(1, 1, "s", slice(96, 128))
             mm_dz1(1, 0)
-            il_adj(1, 1, "v")
-            quant(adj_c[1, 1], adj_s[1, 1], adj_grp[1, 1], E4)
-            mm_dz1(1, 1)
-
-            w_words = w_raw[:].rearrange("p b h f -> p (b h f)").bitcast(F32)
-            d1w = [words_of(dz1[g][:]) for g in range(2)]
-            for t in range(J):
-                cast(0, t, "s")
-            trans("f00", 0, d1w[0], (0, 1))
-            trans("f01", 1, d1w[0], (2, 3))
-            trans("w0", 2, w_words, (0, 1))
-            trans("w1", 3, w_words, (2, 3))
-            for t in range(J):
-                cast(1, t, "v" if t else "v")
-            tr_out("f00", ft_grp[0], 0, "s")
-            tr_out("f01", ft_grp[0], 1, "s")
-            tr_out("w0", w_grp, 0, "s")
-            tr_out("w1", w_grp, 1, "s")
-            trans("f10", 4, d1w[1], (0, 1))
-            trans("f11", 5, d1w[1], (2, 3))
-            il(nd_grp[0], dz1[0], "v")
-            quant(ft_c[0], ft_s[0], ft_grp[0], E5)
-            quant(w_c, w_s, w_grp, E4)
-            tr_out("f10", ft_grp[1], 0, "s")
-            tr_out("f11", ft_grp[1], 1, "s")
-            for t in range(J):
-                mm_dx(0, t, (6, 7, 0, 1)[t])
-            il(nd_grp[1], dz1[1], "v")
-            quant(ft_c[1], ft_s[1], ft_grp[1], E5)
-            for t in range(J):
-                dx_out(0, t, "s")
-            for t in range(J):
-                mm_dx(1, t, (6, 7, 0, 1)[t])
-            quant(nd_c[0], nd_s[0], nd_grp[0], E5)
-            il(x_grp[0], x_raw[0], "v")
-            quant(nd_c[1], nd_s[1], nd_grp[1], E5)
+            cast(0, 0, "v")
+            cast(0, 1, "s")
+            il_adj(1, 1, "v", slice(64, 96))
+            cast(0, 2, "s")
             quant(x_c[0], x_s[0], x_grp[0], E4)
-            for i in range(4):
-                mm_dw(0, i, 2 + i)
-            for i in range(4):
-                dx_out(1, i, "s")
-            il(x_grp[1], x_raw[1], "v")
+            trans("f00", 4, words_of(dz1[0][:]), (0, 1))
+            cast(0, 3, "s")
+            quant(adj_c[1, 1], adj_s[1, 1], adj_grp[1, 1], E4)
+            trans("w1", 5, w_words, (2, 3))
+            tr_out("f00", ft_grp[0], 0, "s")
+            il(nd_grp[0], dz1[0], "v", slice(0, 512))
+            trans("f01", 6, words_of(dz1[0][:]), (2, 3))
+            tr_out("w1", w_grp, 1, "s")
+            trans("w0", 7, w_words, (0, 1))
+            tr_out("f01", ft_grp[0], 1, "s")
+            mm_dz1(1, 1)
+            tr_out("w0", w_grp, 0, "v")
+            cast(1, 0, "s")
+            cast(1, 1, "v")
+            cast(1, 2, "s")
+            quant(ft_c[0], ft_s[0], ft_grp[0], E5)
+            cast(1, 3, "s")
+            trans("f10", 4, words_of(dz1[1][:]), (0, 1))
+            quant(w_c, w_s, w_grp, E4)
+            trans("f11", 5, words_of(dz1[1][:]), (2, 3))
+            tr_out("f10", ft_grp[1], 0, "s")
+            il(nd_grp[1], dz1[1], "v", slice(0, 512))
+            mm_dx(0, 0, 6)
+            mm_dx(0, 1, 7)
+            mm_dx(0, 2, 0)
+            mm_dx(0, 3, 1)
+            tr_out("f11", ft_grp[1], 1, "s")
+            dx_out(0, 0, "s")
+            quant(ft_c[1], ft_s[1], ft_grp[1], E5)
+            dx_out(0, 2, "s")
+            quant(nd_c[1], nd_s[1], nd_grp[1], E5)
+            dx_out(0, 3, "s")
+            mm_dx(1, 0, 2)
+            mm_dx(1, 1, 3)
+            mm_dx(1, 2, 4)
+            mm_dx(1, 3, 5)
+            quant(nd_c[0], nd_s[0], nd_grp[0], E5)
+            dx_out(1, 0, "s")
+            il(x_grp[1], x_raw[1], "v", slice(0, 256))
+            dx_out(1, 1, "s")
+            mm_dw(0, 0, 6)
+            mm_dw(0, 1, 0)
+            mm_dw(0, 2, 1)
+            mm_dw(0, 3, 2)
+            dx_out(1, 2, "s")
             quant(x_c[1], x_s[1], x_grp[1], E4)
-            for i in range(4):
-                mm_dw(1, i, 2 + i)
-            for i in range(4):
-                dw_out(i, "v" if i % 2 else "s")
+            dx_out(1, 3, "s")
+            mm_dw(1, 0, 6)
+            mm_dw(1, 1, 0)
+            mm_dw(1, 2, 1)
+            mm_dw(1, 3, 2)
+            dx_out(0, 1, "s")
+            dw_out(0, "v")
+            dw_out(1, "s")
+            dw_out(2, "v")
+            dw_out(3, "s")

@@ -32,7 +32,7 @@ def tile_gat_pa_v_kernel(tc, x, adj, W0, p, grad_out, out_0, out_1):
         def bank(i, shape, name):
             return ps.tile(shape, F32, name=name, tag="b%d" % i)
 
-        adj_raw = {(k, g): st([P, J, G], BF16, "ar%d%d" % (k, g)) for k in range(2) for g in range(2)}
+        adj_raw = [st([P, J, N], BF16, "ar%d" % k) for k in range(2)]
         adj_grp = {(k, g): st([P, G, J], BF16, "ag%d%d" % (k, g)) for k in range(2) for g in range(2)}
         adj_c = {(k, g): st([P, G], U32, "ac%d%d" % (k, g)) for k in range(2) for g in range(2)}
         adj_s = {(k, g): st([P, G], U8, "as%d%d" % (k, g)) for k in range(2) for g in range(2)}
@@ -46,7 +46,8 @@ def tile_gat_pa_v_kernel(tc, x, adj, W0, p, grad_out, out_0, out_1):
         x_grp = [st([P, NFEAT, J], BF16, "xg%d" % k) for k in range(2)]
         x_c = [st([P, NFEAT], U32, "xc%d" % k) for k in range(2)]
         x_s = [st([P, NFEAT], U8, "xs%d" % k) for k in range(2)]
-        w_raw = st([P, 4, NHEADS, NHID], BF16, "wr")
+        w_raw = st([P, NHEADS, 4 * NHID], BF16, "wr")
+        w_srt = st([P, 4, 2, P], F32, "wsrt")
         w_grp = st([P, NFEAT, J], BF16, "wg")
         w_c = st([P, NFEAT], U32, "wc")
         w_s = st([P, NFEAT], U8, "ws")
@@ -57,15 +58,14 @@ def tile_gat_pa_v_kernel(tc, x, adj, W0, p, grad_out, out_0, out_1):
         ft_grp = [st([P, G, J], BF16, "fg%d" % g) for g in range(2)]
         ft_c = [st([P, G], U32, "fc%d" % g) for g in range(2)]
         ft_s = [st([P, G], U8, "fs%d" % g) for g in range(2)]
-        dx = {(g, t): st([P, NFEAT], F32, "dx%d%d" % (g, t)) for g in range(2) for t in range(J)}
-        dw = [st([P, C], F32, "dw%d" % i) for i in range(4)]
+        dx = [st([P, J, NFEAT], F32, "dx%d" % g) for g in range(2)]
+        dw = st([P, NHEADS, 4, NHID], F32, "dw")
         ident = st([P, P], F32, "ident")
         warm = st([P, 1], F32, "warm")
 
-        def load_adj(k, g):
+        def load_adj(k, cols):
             nc.sync.dma_start(
-                out=adj_raw[k, g][:],
-                in_=adj[G * k : G * (k + 1), G * g : G * (g + 1)].rearrange("(p j) w -> p j w", j=J),
+                out=adj_raw[k][:, :, cols], in_=adj[G * k : G * (k + 1), cols].rearrange("(p j) w -> p j w", j=J)
             )
 
         def load_p(k):
@@ -78,8 +78,7 @@ def tile_gat_pa_v_kernel(tc, x, adj, W0, p, grad_out, out_0, out_1):
             nc.sync.dma_start(out=x_raw[k][:], in_=x[G * k : G * (k + 1), :].rearrange("(p j) w -> p j w", j=J))
 
         def load_w():
-            for h in range(NHEADS):
-                nc.sync.dma_start(out=w_raw[:, :, h, :], in_=W0[h].rearrange("(b p) f -> p b f", p=P))
+            nc.sync.dma_start(out=w_raw[:], in_=W0.rearrange("h (p b) f -> p h (b f)", b=4))
 
         def exp_p(k, h):
             nc.scalar.activation(
@@ -106,14 +105,32 @@ def tile_gat_pa_v_kernel(tc, x, adj, W0, p, grad_out, out_0, out_1):
                 nc.scalar.copy(out=out, in_=in_)
 
         def il_adj(k, g, engine, m):
-            dst = adj_grp[k, g][:].rearrange("p (t m) j -> p m j t", t=J)[:, m]
-            src = adj_raw[k, g][:].rearrange("p j (m t) -> p m j t", t=J)[:, m]
-            copy(engine, dst, src)
+            copy(
+                engine,
+                adj_grp[k, g][:].rearrange("p (t m) j -> p m j t", t=J)[:, m],
+                adj_raw[k][:, :, G * g : G * (g + 1)].rearrange("p j (m t) -> p m j t", t=J)[:, m],
+            )
 
         def il(grp, raw, engine, c=slice(0, 512)):
-            dst = grp[:, c, :].rearrange("p (c i) t -> p c t i", i=4)
-            s = raw[:, :, c].rearrange("p t (c i) -> p c t i", i=4)
-            copy(engine, dst, s)
+            copy(
+                engine,
+                grp[:, c, :].rearrange("p (c i) t -> p c t i", i=4),
+                raw[:, :, c].rearrange("p t (c i) -> p c t i", i=4),
+            )
+
+        def il_x(k, engine, m):
+            copy(
+                engine,
+                x_grp[k][:].rearrange("p (t m) j -> p m j t", t=J)[:, m],
+                x_raw[k][:].rearrange("p j (m t) -> p m j t", t=J)[:, m],
+            )
+
+        def sort_w(engine):
+            copy(
+                engine,
+                w_srt[:].rearrange("p b u (h q) -> p b h q u", h=NHEADS),
+                w_raw[:].rearrange("p h w -> p (h w)").bitcast(F32).rearrange("p (h b q u) -> p b h q u", h=NHEADS, b=4, u=2),
+            )
 
         def quant(codes, scales, grp, fmt):
             nc.vector.quantize_mx(out=codes[:].bitcast(fmt), scales=scales[:], in_=grp[:].rearrange("p c j -> p (c j)"))
@@ -140,12 +157,12 @@ def tile_gat_pa_v_kernel(tc, x, adj, W0, p, grad_out, out_0, out_1):
 
         tr = {}
 
-        def trans(key, b, raw_words, blocks):
+        def trans(key, b, words, blocks):
             t_ps = bank(b, [P, 2, 2, P], "tr_%s" % key)
             tr[key] = t_ps
             for a, blk in enumerate(blocks):
                 for u in range(2):
-                    nc.tensor.transpose(t_ps[:, a, u, :], raw_words[:, 256 * blk + u : 256 * (blk + 1) : 2], ident[:])
+                    nc.tensor.transpose(t_ps[:, a, u, :], words(blk, u), ident[:])
 
         def tr_out(key, grp, half, engine):
             words = grp[:].rearrange("p c j -> p (c j)").bitcast(F32)
@@ -155,8 +172,12 @@ def tile_gat_pa_v_kernel(tc, x, adj, W0, p, grad_out, out_0, out_1):
                 tr[key][:].rearrange("p a u r -> p a r u"),
             )
 
-        def words_of(tile3):
-            return tile3.rearrange("p a b -> p (a b)").bitcast(F32)
+        def dz1_words(g):
+            w = dz1[g][:].rearrange("p t c -> p (t c)").bitcast(F32)
+            return lambda blk, u: w[:, 256 * blk + u : 256 * (blk + 1) : 2]
+
+        def w_words(blk, u):
+            return w_srt[:, blk, u, :]
 
         def mm_dx(g, t, b):
             o = bank(b, [P, NFEAT], "dxp%d%d" % (g, t))
@@ -173,9 +194,16 @@ def tile_gat_pa_v_kernel(tc, x, adj, W0, p, grad_out, out_0, out_1):
             )
 
         def dx_out(g, t, engine):
-            copy(engine, dx[g, t][:], acc["dx", g, t][:])
+            copy(
+                engine,
+                dx[g][:, t, :].rearrange("p (q b) -> p q b", b=4),
+                acc["dx", g, t][:].rearrange("p (b q) -> p q b", b=4),
+            )
+
+        def dx_store(g, h):
+            t = slice(2 * h, 2 * h + 2)
             nc.sync.dma_start(
-                out=out_0[G * g : G * (g + 1), :].rearrange("(m t) w -> m t w", t=J)[:, t, :], in_=dx[g, t][:]
+                out=out_0[G * g : G * (g + 1), :].rearrange("(m t) w -> m t w", t=J)[:, t, :], in_=dx[g][:, t, :]
             )
 
         def mm_dw(k, i, b):
@@ -193,119 +221,109 @@ def tile_gat_pa_v_kernel(tc, x, adj, W0, p, grad_out, out_0, out_1):
             )
 
         def dw_out(i, engine):
-            copy(engine, dw[i][:], acc["dw", i][:])
+            copy(engine, dw[:, :, i, :], acc["dw", i][:].rearrange("p (h f) -> p h f", h=NHEADS))
+
+        def dw_store(h):
             nc.sync.dma_start(
-                out=out_1[:, P * i : P * (i + 1), :].rearrange("h i f -> i h f"),
-                in_=dw[i][:].rearrange("p (h f) -> p h f", h=NHEADS),
+                out=out_1.rearrange("h (m b) f -> m h b f", b=4)[:, :, 2 * h : 2 * h + 2, :], in_=dw[:, :, 2 * h : 2 * h + 2, :]
             )
 
-        w_words = w_raw[:].rearrange("p b h f -> p (b h f)").bitcast(F32)
         with tc.manual_schedule():
             nc.vector.memset(warm[:], 0.0)
             nc.scalar.activation(out=warm[:], in_=warm[:], func=ACT.Exp)
             make_identity(nc, ident[:])
 
+            load_adj(0, slice(0, N))
+            load_adj(1, slice(0, G))
             load_p(0)
             load_g(0)
             load_p(1)
             load_g(1)
-            load_adj(0, 1)
-            load_adj(0, 0)
-            load_x(0)
-            load_adj(1, 0)
-            load_adj(1, 1)
-            load_x(1)
             load_w()
+            load_adj(1, slice(G, N))
+            load_x(0)
+            load_x(1)
 
+            il_adj(0, 0, "v", slice(0, 128))
+            il_adj(1, 0, "v", slice(0, 128))
+            quant(adj_c[0, 0], adj_s[0, 0], adj_grp[0, 0], E4)
+            il_adj(0, 1, "v", slice(0, 64))
             exp_p(0, 0)
+            quant(adj_c[1, 0], adj_s[1, 0], adj_grp[1, 0], E4)
             exp_p(0, 1)
             mul(0, 0)
             mul(0, 1)
-            exp_p(1, 1)
-            quant(dz2_c[0], dz2_s[0], dz2[0], E5)
+            il_adj(0, 1, "v", slice(64, 128))
             exp_p(1, 0)
-            mul(1, 1)
-            il_adj(0, 1, "s", slice(32, 96))
-            il_adj(0, 1, "v", slice(0, 32))
-            il_adj(0, 1, "v", slice(96, 128))
+            quant(dz2_c[0], dz2_s[0], dz2[0], E5)
+            mm_dz1(0, 0, (0, 1, 2, 3))
+            exp_p(1, 1)
             mul(1, 0)
-            il_adj(0, 0, "s", slice(32, 96))
-            il_adj(0, 0, "v", slice(96, 128))
-            il_adj(0, 0, "v", slice(0, 32))
+            mul(1, 1)
             quant(adj_c[0, 1], adj_s[0, 1], adj_grp[0, 1], E4)
-            il(x_grp[0], x_raw[0], "s", slice(256, 512))
-            quant(adj_c[0, 0], adj_s[0, 0], adj_grp[0, 0], E4)
-            mm_dz1(0, 1, (0, 1, 2, 3))
+            sort_w("s")
+            trans("w0", 4, w_words, (0, 1))
             quant(dz2_c[1], dz2_s[1], dz2[1], E5)
-            il_adj(1, 0, "s", slice(0, 32))
-            il_adj(1, 0, "v", slice(32, 64))
-            mm_dz1(0, 0, (4, 5, 6, 7))
-            il_adj(1, 0, "s", slice(64, 96))
-            il_adj(1, 0, "v", slice(96, 128))
-            il(x_grp[0], x_raw[0], "v", slice(0, 256))
-            il_adj(1, 1, "s", slice(0, 64))
-            quant(adj_c[1, 0], adj_s[1, 0], adj_grp[1, 0], E4)
-            il(x_grp[1], x_raw[1], "v", slice(256, 512))
-            il_adj(1, 1, "s", slice(96, 128))
             mm_dz1(1, 0)
-            cast(0, 0, "v")
+            tr_out("w0", w_grp, 0, "s")
+            il_adj(1, 1, "v", slice(0, 128))
+            cast(0, 0, "s")
             cast(0, 1, "s")
-            il_adj(1, 1, "v", slice(64, 96))
             cast(0, 2, "s")
-            quant(x_c[0], x_s[0], x_grp[0], E4)
-            trans("f00", 4, words_of(dz1[0][:]), (0, 1))
             cast(0, 3, "s")
-            quant(adj_c[1, 1], adj_s[1, 1], adj_grp[1, 1], E4)
             trans("w1", 5, w_words, (2, 3))
-            tr_out("f00", ft_grp[0], 0, "s")
-            il(nd_grp[0], dz1[0], "v", slice(0, 512))
-            trans("f01", 6, words_of(dz1[0][:]), (2, 3))
-            tr_out("w1", w_grp, 1, "s")
-            trans("w0", 7, w_words, (0, 1))
-            tr_out("f01", ft_grp[0], 1, "s")
+            trans("f00", 6, dz1_words(0), (0, 1))
+            il_x(0, "v", slice(0, 64))
+            quant(adj_c[1, 1], adj_s[1, 1], adj_grp[1, 1], E4)
+            il_x(0, "v", slice(64, 128))
+            trans("f01", 7, dz1_words(0), (2, 3))
+            mm_dz1(0, 1, (0, 1, 2, 3))
             mm_dz1(1, 1)
-            tr_out("w0", w_grp, 0, "v")
+            tr_out("w1", w_grp, 1, "s")
+            tr_out("f00", ft_grp[0], 0, "s")
+            tr_out("f01", ft_grp[0], 1, "s")
+            il(nd_grp[0], dz1[0], "v", slice(0, 512))
+            quant(w_c, w_s, w_grp, E4)
+            quant(ft_c[0], ft_s[0], ft_grp[0], E5)
+            for t in range(J):
+                mm_dx(0, t, 4 + t)
             cast(1, 0, "s")
             cast(1, 1, "v")
             cast(1, 2, "s")
-            quant(ft_c[0], ft_s[0], ft_grp[0], E5)
-            cast(1, 3, "s")
-            trans("f10", 4, words_of(dz1[1][:]), (0, 1))
-            quant(w_c, w_s, w_grp, E4)
-            trans("f11", 5, words_of(dz1[1][:]), (2, 3))
-            tr_out("f10", ft_grp[1], 0, "s")
-            il(nd_grp[1], dz1[1], "v", slice(0, 512))
-            mm_dx(0, 0, 6)
-            mm_dx(0, 1, 7)
-            mm_dx(0, 2, 0)
-            mm_dx(0, 3, 1)
-            tr_out("f11", ft_grp[1], 1, "s")
+            cast(1, 3, "v")
+            trans("f10", 0, dz1_words(1), (0, 1))
+            trans("f11", 1, dz1_words(1), (2, 3))
             dx_out(0, 0, "s")
-            quant(ft_c[1], ft_s[1], ft_grp[1], E5)
-            dx_out(0, 2, "s")
-            quant(nd_c[1], nd_s[1], nd_grp[1], E5)
-            dx_out(0, 3, "s")
-            mm_dx(1, 0, 2)
-            mm_dx(1, 1, 3)
-            mm_dx(1, 2, 4)
-            mm_dx(1, 3, 5)
-            quant(nd_c[0], nd_s[0], nd_grp[0], E5)
-            dx_out(1, 0, "s")
-            il(x_grp[1], x_raw[1], "v", slice(0, 256))
-            dx_out(1, 1, "s")
-            mm_dw(0, 0, 6)
-            mm_dw(0, 1, 0)
-            mm_dw(0, 2, 1)
-            mm_dw(0, 3, 2)
-            dx_out(1, 2, "s")
-            quant(x_c[1], x_s[1], x_grp[1], E4)
-            dx_out(1, 3, "s")
-            mm_dw(1, 0, 6)
-            mm_dw(1, 1, 0)
-            mm_dw(1, 2, 1)
-            mm_dw(1, 3, 2)
             dx_out(0, 1, "s")
+            dx_store(0, 0)
+            quant(x_c[0], x_s[0], x_grp[0], E4)
+            quant(nd_c[0], nd_s[0], nd_grp[0], E5)
+            il(nd_grp[1], dz1[1], "v", slice(0, 256))
+            tr_out("f10", ft_grp[1], 0, "s")
+            tr_out("f11", ft_grp[1], 1, "s")
+            dx_out(0, 2, "s")
+            dx_out(0, 3, "s")
+            dx_store(0, 1)
+            quant(ft_c[1], ft_s[1], ft_grp[1], E5)
+            for t in range(J):
+                mm_dx(1, t, (0, 1, 6, 7)[t])
+            for i in range(4):
+                mm_dw(0, i, (2, 3, 4, 5)[i])
+            il(nd_grp[1], dz1[1], "v", slice(256, 512))
+            il_x(1, "v", slice(0, 128))
+            quant(nd_c[1], nd_s[1], nd_grp[1], E5)
+            quant(x_c[1], x_s[1], x_grp[1], E4)
+            dx_out(1, 0, "s")
+            dx_out(1, 1, "s")
+            dx_store(1, 0)
+            dx_out(1, 2, "s")
+            dx_out(1, 3, "s")
+            dx_store(1, 1)
+            for i in range(4):
+                mm_dw(1, i, 0)
             dw_out(0, "v")
             dw_out(1, "s")
+            dw_store(0)
             dw_out(2, "v")
             dw_out(3, "s")
+            dw_store(1)

@@ -32,7 +32,9 @@ def tile_gat_pa_v_kernel(tc, x, adj, W0, p, grad_out, out_0, out_1):
         def bank(i, shape, name):
             return ps.tile(shape, F32, name=name, tag="b%d" % i)
 
-        adj_raw = [st([P, J, N], BF16, "ar%d" % k) for k in range(2)]
+        adj_raw0 = st([P, J, N], BF16, "ar0")
+        adj_raw1 = [st([P, J, G], BF16, "ar1%d" % g) for g in range(2)]
+        adj_raw = {(0, 0): adj_raw0[:, :, :G], (0, 1): adj_raw0[:, :, G:], (1, 0): adj_raw1[0][:], (1, 1): adj_raw1[1][:]}
         adj_grp = {(k, g): st([P, G, J], BF16, "ag%d%d" % (k, g)) for k in range(2) for g in range(2)}
         adj_c = {(k, g): st([P, G], U32, "ac%d%d" % (k, g)) for k in range(2) for g in range(2)}
         adj_s = {(k, g): st([P, G], U8, "as%d%d" % (k, g)) for k in range(2) for g in range(2)}
@@ -59,13 +61,16 @@ def tile_gat_pa_v_kernel(tc, x, adj, W0, p, grad_out, out_0, out_1):
         ft_c = [st([P, G], U32, "fc%d" % g) for g in range(2)]
         ft_s = [st([P, G], U8, "fs%d" % g) for g in range(2)]
         dx = [st([P, J, NFEAT], F32, "dx%d" % g) for g in range(2)]
-        dw = st([P, NHEADS, 4, NHID], F32, "dw")
+        dw = [st([P, NHEADS, 2, NHID], F32, "dw%d" % i) for i in range(2)]
         ident = st([P, P], F32, "ident")
         warm = st([P, 1], F32, "warm")
 
-        def load_adj(k, cols):
+        def load_adj0():
+            nc.sync.dma_start(out=adj_raw0[:], in_=adj[:G, :].rearrange("(p j) w -> p j w", j=J))
+
+        def load_adj1(g):
             nc.sync.dma_start(
-                out=adj_raw[k][:, :, cols], in_=adj[G * k : G * (k + 1), cols].rearrange("(p j) w -> p j w", j=J)
+                out=adj_raw1[g][:], in_=adj[G:, G * g : G * (g + 1)].rearrange("(p j) w -> p j w", j=J)
             )
 
         def load_p(k):
@@ -104,11 +109,11 @@ def tile_gat_pa_v_kernel(tc, x, adj, W0, p, grad_out, out_0, out_1):
             else:
                 nc.scalar.copy(out=out, in_=in_)
 
-        def il_adj(k, g, engine, m):
+        def il_adj(k, g, engine, t0, t1):
             copy(
                 engine,
-                adj_grp[k, g][:].rearrange("p (t m) j -> p m j t", t=J)[:, m],
-                adj_raw[k][:, :, G * g : G * (g + 1)].rearrange("p j (m t) -> p m j t", t=J)[:, m],
+                adj_grp[k, g][:].rearrange("p (t m) j -> p m j t", t=J)[:, :, :, t0:t1],
+                adj_raw[k, g].rearrange("p j (m t) -> p m j t", t=J)[:, :, :, t0:t1],
             )
 
         def il(grp, raw, engine, c=slice(0, 512)):
@@ -221,11 +226,11 @@ def tile_gat_pa_v_kernel(tc, x, adj, W0, p, grad_out, out_0, out_1):
             )
 
         def dw_out(i, engine):
-            copy(engine, dw[:, :, i, :], acc["dw", i][:].rearrange("p (h f) -> p h f", h=NHEADS))
+            copy(engine, dw[i // 2][:, :, i % 2, :], acc["dw", i][:].rearrange("p (h f) -> p h f", h=NHEADS))
 
         def dw_store(h):
             nc.sync.dma_start(
-                out=out_1.rearrange("h (m b) f -> m h b f", b=4)[:, :, 2 * h : 2 * h + 2, :], in_=dw[:, :, 2 * h : 2 * h + 2, :]
+                out=out_1.rearrange("h (m b) f -> m h b f", b=4)[:, :, 2 * h : 2 * h + 2, :], in_=dw[h][:]
             )
 
         with tc.manual_schedule():
@@ -233,97 +238,101 @@ def tile_gat_pa_v_kernel(tc, x, adj, W0, p, grad_out, out_0, out_1):
             nc.scalar.activation(out=warm[:], in_=warm[:], func=ACT.Exp)
             make_identity(nc, ident[:])
 
-            load_adj(0, slice(0, N))
-            load_adj(1, slice(0, G))
+            load_adj0()
             load_p(0)
             load_g(0)
             load_p(1)
             load_g(1)
+            load_adj1(0)
+            load_adj1(1)
             load_w()
-            load_adj(1, slice(G, N))
             load_x(0)
             load_x(1)
 
-            il_adj(0, 0, "v", slice(0, 128))
-            il_adj(1, 0, "v", slice(0, 128))
+            il_adj(0, 0, "s", 3, 4)
+            il_adj(0, 1, "s", 2, 4)
+            il_adj(0, 0, "v", 0, 3)
+            il_adj(0, 1, "v", 0, 2)
             quant(adj_c[0, 0], adj_s[0, 0], adj_grp[0, 0], E4)
-            il_adj(0, 1, "v", slice(0, 64))
+            quant(adj_c[0, 1], adj_s[0, 1], adj_grp[0, 1], E4)
             exp_p(0, 0)
-            quant(adj_c[1, 0], adj_s[1, 0], adj_grp[1, 0], E4)
             exp_p(0, 1)
             mul(0, 0)
             mul(0, 1)
-            il_adj(0, 1, "v", slice(64, 128))
             exp_p(1, 0)
+            exp_p(1, 1)
             quant(dz2_c[0], dz2_s[0], dz2[0], E5)
             mm_dz1(0, 0, (0, 1, 2, 3))
-            exp_p(1, 1)
+            mm_dz1(0, 1, (4, 5, 6, 7))
             mul(1, 0)
             mul(1, 1)
-            quant(adj_c[0, 1], adj_s[0, 1], adj_grp[0, 1], E4)
-            sort_w("s")
-            trans("w0", 4, w_words, (0, 1))
+            il_adj(1, 0, "s", 1, 4)
+            il_adj(1, 0, "v", 0, 1)
             quant(dz2_c[1], dz2_s[1], dz2[1], E5)
+            il_adj(1, 1, "s", 1, 4)
+            il_adj(1, 1, "v", 0, 1)
+            quant(adj_c[1, 0], adj_s[1, 0], adj_grp[1, 0], E4)
             mm_dz1(1, 0)
-            tr_out("w0", w_grp, 0, "s")
-            il_adj(1, 1, "v", slice(0, 128))
+            sort_w("v")
+            quant(adj_c[1, 1], adj_s[1, 1], adj_grp[1, 1], E4)
             cast(0, 0, "s")
             cast(0, 1, "s")
+            trans("w0", 0, w_words, (0, 1))
+            mm_dz1(1, 1)
             cast(0, 2, "s")
             cast(0, 3, "s")
-            trans("w1", 5, w_words, (2, 3))
-            trans("f00", 6, dz1_words(0), (0, 1))
-            il_x(0, "v", slice(0, 64))
-            quant(adj_c[1, 1], adj_s[1, 1], adj_grp[1, 1], E4)
             il_x(0, "v", slice(64, 128))
-            trans("f01", 7, dz1_words(0), (2, 3))
-            mm_dz1(0, 1, (0, 1, 2, 3))
-            mm_dz1(1, 1)
-            tr_out("w1", w_grp, 1, "s")
-            tr_out("f00", ft_grp[0], 0, "s")
-            tr_out("f01", ft_grp[0], 1, "s")
-            il(nd_grp[0], dz1[0], "v", slice(0, 512))
-            quant(w_c, w_s, w_grp, E4)
-            quant(ft_c[0], ft_s[0], ft_grp[0], E5)
-            for t in range(J):
-                mm_dx(0, t, 4 + t)
-            cast(1, 0, "s")
-            cast(1, 1, "v")
-            cast(1, 2, "s")
+            il_x(1, "v", slice(0, 128))
+            trans("f00", 1, dz1_words(0), (0, 1))
+            trans("f01", 2, dz1_words(0), (2, 3))
+            trans("w1", 3, w_words, (2, 3))
+            tr_out("w0", w_grp, 0, "s")
             cast(1, 3, "v")
-            trans("f10", 0, dz1_words(1), (0, 1))
-            trans("f11", 1, dz1_words(1), (2, 3))
+            tr_out("f00", ft_grp[0], 0, "v")
+            cast(1, 1, "s")
+            cast(1, 2, "s")
+            tr_out("f01", ft_grp[0], 1, "s")
+            tr_out("w1", w_grp, 1, "s")
+            cast(1, 0, "s")
+            trans("f11", 5, dz1_words(1), (2, 3))
+            trans("f10", 6, dz1_words(1), (0, 1))
+            il(nd_grp[0], dz1[0], "v", slice(0, 256))
+            quant(ft_c[0], ft_s[0], ft_grp[0], E5)
+            quant(w_c, w_s, w_grp, E4)
+            for t in range(J):
+                mm_dx(0, t, (0, 1, 7, 4)[t])
+            tr_out("f11", ft_grp[1], 1, "s")
+            tr_out("f10", ft_grp[1], 0, "s")
+            il_x(0, "v", slice(0, 64))
+            il(nd_grp[1], dz1[1], "v", slice(256, 512))
+            il(nd_grp[0], dz1[0], "v", slice(256, 512))
+            quant(ft_c[1], ft_s[1], ft_grp[1], E5)
             dx_out(0, 0, "s")
             dx_out(0, 1, "s")
             dx_store(0, 0)
-            quant(x_c[0], x_s[0], x_grp[0], E4)
-            quant(nd_c[0], nd_s[0], nd_grp[0], E5)
-            il(nd_grp[1], dz1[1], "v", slice(0, 256))
-            tr_out("f10", ft_grp[1], 0, "s")
-            tr_out("f11", ft_grp[1], 1, "s")
             dx_out(0, 2, "s")
             dx_out(0, 3, "s")
             dx_store(0, 1)
-            quant(ft_c[1], ft_s[1], ft_grp[1], E5)
             for t in range(J):
-                mm_dx(1, t, (0, 1, 6, 7)[t])
+                mm_dx(1, t, (2, 3, 5, 6)[t])
+            quant(nd_c[0], nd_s[0], nd_grp[0], E5)
+            quant(x_c[0], x_s[0], x_grp[0], E4)
             for i in range(4):
-                mm_dw(0, i, (2, 3, 4, 5)[i])
-            il(nd_grp[1], dz1[1], "v", slice(256, 512))
-            il_x(1, "v", slice(0, 128))
-            quant(nd_c[1], nd_s[1], nd_grp[1], E5)
+                mm_dw(0, i, (0, 1, 7, 4)[i])
+            il(nd_grp[1], dz1[1], "v", slice(0, 256))
             quant(x_c[1], x_s[1], x_grp[1], E4)
+            quant(nd_c[1], nd_s[1], nd_grp[1], E5)
             dx_out(1, 0, "s")
             dx_out(1, 1, "s")
             dx_store(1, 0)
             dx_out(1, 2, "s")
             dx_out(1, 3, "s")
             dx_store(1, 1)
-            for i in range(4):
+            for i in (0, 2, 1, 3):
                 mm_dw(1, i, 0)
             dw_out(0, "v")
-            dw_out(1, "s")
+            dw_out(2, "s")
+            dw_out(1, "v")
             dw_store(0)
-            dw_out(2, "v")
             dw_out(3, "s")
             dw_store(1)

from contextlib import ExitStack

import concourse.mybir as mybir
from concourse.masks import make_identity

N, NFEAT, NHEADS, NHID = 1024, 512, 4, 128
C = NHEADS * NHID
P = 128
J = 4
G = 512
FLOPS = 2 * N * N * C + 2 * 2 * N * NFEAT * C
BYTES = 2 * (N * NFEAT + N * N + NFEAT * C + N * C) + 4 * N * C + 4 * (N * NFEAT + NFEAT * C)

F32 = mybir.dt.float32
BF16 = mybir.dt.bfloat16
U32 = mybir.dt.uint32
U8 = mybir.dt.uint8
E4 = mybir.dt.float8_e4m3fn_x4
E5 = mybir.dt.float8_e5m2_x4
ACT = mybir.ActivationFunctionType
ALU = mybir.AluOpType

def tile_gat_pa_v_kernel(tc, x, adj, W0, p, grad_out, out_0, out_1):
    nc = tc.nc
    with ExitStack() as ctx:
        sb = ctx.enter_context(tc.tile_pool(name="sb", bufs=1))
        ps = ctx.enter_context(tc.psum_pool(name="ps", bufs=1))

        def st(shape, dtype, name):
            return sb.tile(shape, dtype, name=name, tag=name, align_bytes=256)

        def bank(i, shape, name):
            return ps.tile(shape, F32, name=name, tag="b%d" % i)

        adj_raw0 = st([P, J, N], BF16, "ar0")
        adj_raw1 = [st([P, J, G], BF16, "ar1%d" % g) for g in range(2)]
        adj_raw = {(0, 0): adj_raw0[:, :, :G], (0, 1): adj_raw0[:, :, G:], (1, 0): adj_raw1[0][:], (1, 1): adj_raw1[1][:]}
        adj_grp = {(k, g): st([P, G, J], BF16, "ag%d%d" % (k, g)) for k in range(2) for g in range(2)}
        adj_c = {(k, g): st([P, G], U32, "ac%d%d" % (k, g)) for k in range(2) for g in range(2)}
        adj_s = {(k, g): st([P, G], U8, "as%d%d" % (k, g)) for k in range(2) for g in range(2)}
        p_raw = [st([P, J, C], F32, "pr%d" % k) for k in range(2)]
        e_grp = {(k, h): st([P, C // 2, J], F32, "eg%d%d" % (k, h)) for k in range(2) for h in range(2)}
        g_raw = [st([P, J, C], BF16, "gr%d" % k) for k in range(2)]
        dz2 = [st([P, C, J], BF16, "dz%d" % k) for k in range(2)]
        dz2_c = [st([P, C], U32, "dc%d" % k) for k in range(2)]
        dz2_s = [st([P, C], U8, "ds%d" % k) for k in range(2)]
        x_raw = [st([P, J, NFEAT], BF16, "xr%d" % k) for k in range(2)]
        x_grp = [st([P, NFEAT, J], BF16, "xg%d" % k) for k in range(2)]
        x_c = [st([P, NFEAT], U32, "xc%d" % k) for k in range(2)]
        x_s = [st([P, NFEAT], U8, "xs%d" % k) for k in range(2)]
        w_raw = st([P, NHEADS, 4 * NHID], BF16, "wr")
        w_srt = st([P, 4, 2, P], F32, "wsrt")
        w_grp = st([P, NFEAT, J], BF16, "wg")
        w_c = st([P, NFEAT], U32, "wc")
        w_s = st([P, NFEAT], U8, "ws")
        dz1 = [st([P, J, C], BF16, "d1%d" % g) for g in range(2)]
        nd_grp = [st([P, C, J], BF16, "ng%d" % g) for g in range(2)]
        nd_c = [st([P, C], U32, "nc%d" % g) for g in range(2)]
        nd_s = [st([P, C], U8, "ns%d" % g) for g in range(2)]
        ft_grp = [st([P, G, J], BF16, "fg%d" % g) for g in range(2)]
        ft_c = [st([P, G], U32, "fc%d" % g) for g in range(2)]
        ft_s = [st([P, G], U8, "fs%d" % g) for g in range(2)]
        dx = [st([P, J, NFEAT], F32, "dx%d" % g) for g in range(2)]
        dw = [st([P, NHEADS, 2, NHID], F32, "dw%d" % i) for i in range(2)]
        ident = st([P, P], F32, "ident")
        warm = st([P, 1], F32, "warm")

        def load_adj0():
            nc.sync.dma_start(out=adj_raw0[:], in_=adj[:G, :].rearrange("(p j) w -> p j w", j=J))

        def load_adj1(g):
            nc.sync.dma_start(
                out=adj_raw1[g][:], in_=adj[G:, G * g : G * (g + 1)].rearrange("(p j) w -> p j w", j=J)
            )

        def load_p(k):
            nc.sync.dma_start(out=p_raw[k][:], in_=p[G * k : G * (k + 1), :].rearrange("(p j) w -> p j w", j=J))

        def load_g(k):
            nc.sync.dma_start(out=g_raw[k][:], in_=grad_out[G * k : G * (k + 1), :].rearrange("(p j) w -> p j w", j=J))

        def load_x(k):
            nc.sync.dma_start(out=x_raw[k][:], in_=x[G * k : G * (k + 1), :].rearrange("(p j) w -> p j w", j=J))

        def load_w():
            nc.sync.dma_start(out=w_raw[:], in_=W0.rearrange("h (p b) f -> p h (b f)", b=4))

        def exp_p(k, h):
            nc.scalar.activation(
                out=e_grp[k, h][:].rearrange("p (c i) t -> p c t i", i=4),
                in_=p_raw[k][:, :, 256 * h : 256 * (h + 1)].rearrange("p t (c i) -> p c t i", i=4),
                func=ACT.Exp,
            )

        def mul(k, h):
            c = slice(256 * h, 256 * (h + 1))
            nc.vector.scalar_tensor_tensor(
                out=dz2[k][:, c, :],
                in0=e_grp[k, h][:],
                scalar=1.0,
                in1=g_raw[k][:, :, c].rearrange("p t c -> p c t"),
                op0=ALU.min,
                op1=ALU.mult,
            )

        def copy(engine, out, in_):
            if engine == "v":
                nc.vector.tensor_copy(out=out, in_=in_)
            else:
                nc.scalar.copy(out=out, in_=in_)

        def il_adj(k, g, engine, t0, t1):
            copy(
                engine,
                adj_grp[k, g][:].rearrange("p (t m) j -> p m j t", t=J)[:, :, :, t0:t1],
                adj_raw[k, g].rearrange("p j (m t) -> p m j t", t=J)[:, :, :, t0:t1],
            )

        def il(grp, raw, engine, c=slice(0, 512)):
            copy(
                engine,
                grp[:, c, :].rearrange("p (c i) t -> p c t i", i=4),
                raw[:, :, c].rearrange("p t (c i) -> p c t i", i=4),
            )

        def il_x(k, engine, m):
            copy(
                engine,
                x_grp[k][:].rearrange("p (t m) j -> p m j t", t=J)[:, m],
                x_raw[k][:].rearrange("p j (m t) -> p m j t", t=J)[:, m],
            )

        def sort_w(engine):
            copy(
                engine,
                w_srt[:].rearrange("p b u (h q) -> p b h q u", h=NHEADS),
                w_raw[:].rearrange("p h w -> p (h w)").bitcast(F32).rearrange("p (h b q u) -> p b h q u", h=NHEADS, b=4, u=2),
            )

        def quant(codes, scales, grp, fmt):
            nc.vector.quantize_mx(out=codes[:].bitcast(fmt), scales=scales[:], in_=grp[:].rearrange("p c j -> p (c j)"))

        acc = {}

        def mm_dz1(k, g, banks=None):
            for t in range(J):
                if k == 0:
                    acc[g, t] = bank(banks[t], [P, C], "acc%d%d" % (g, t))
                m = slice(P * t, P * (t + 1))
                nc.tensor.matmul_mx(
                    out=acc[g, t][:],
                    lhsT=adj_c[k, g][:, m].bitcast(E4),
                    lhsT_scale=adj_s[k, g][:, m],
                    rhs=dz2_c[k][:].bitcast(E5),
                    rhs_scale=dz2_s[k][:],
                    start=(k == 0),
                    stop=(k == 1),
                )

        def cast(g, t, engine):
            copy(engine, dz1[g][:, t, :], acc[g, t][:])

        tr = {}

        def trans(key, b, words, blocks):
            t_ps = bank(b, [P, 2, 2, P], "tr_%s" % key)
            tr[key] = t_ps
            for a, blk in enumerate(blocks):
                for u in range(2):
                    nc.tensor.transpose(t_ps[:, a, u, :], words(blk, u), ident[:])

        def tr_out(key, grp, half, engine):
            words = grp[:].rearrange("p c j -> p (c j)").bitcast(F32)
            copy(
                engine,
                words[:, 512 * half : 512 * (half + 1)].rearrange("p (a r u) -> p a r u", a=2, u=2),
                tr[key][:].rearrange("p a u r -> p a r u"),
            )

        def dz1_words(g):
            w = dz1[g][:].rearrange("p t c -> p (t c)").bitcast(F32)
            return lambda blk, u: w[:, 256 * blk + u : 256 * (blk + 1) : 2]

        def w_words(blk, u):
            return w_srt[:, blk, u, :]

        def mm_dx(g, t, b):
            o = bank(b, [P, NFEAT], "dxp%d%d" % (g, t))
            acc["dx", g, t] = o
            m = slice(P * t, P * (t + 1))
            nc.tensor.matmul_mx(
                out=o[:],
                lhsT=ft_c[g][:, m].bitcast(E5),
                lhsT_scale=ft_s[g][:, m],
                rhs=w_c[:].bitcast(E4),
                rhs_scale=w_s[:],
                start=True,
                stop=True,
            )

        def dx_out(g, t, engine):
            copy(
                engine,
                dx[g][:, t, :].rearrange("p (q b) -> p q b", b=4),
                acc["dx", g, t][:].rearrange("p (b q) -> p q b", b=4),
            )

        def dx_store(g, h):
            t = slice(2 * h, 2 * h + 2)
            nc.sync.dma_start(
                out=out_0[G * g : G * (g + 1), :].rearrange("(m t) w -> m t w", t=J)[:, t, :], in_=dx[g][:, t, :]
            )

        def mm_dw(k, i, b):
            if k == 0:
                acc["dw", i] = bank(b, [P, C], "dwp%d" % i)
            m = slice(P * i, P * (i + 1))
            nc.tensor.matmul_mx(
                out=acc["dw", i][:],
                lhsT=x_c[k][:, m].bitcast(E4),
                lhsT_scale=x_s[k][:, m],
                rhs=nd_c[k][:].bitcast(E5),
                rhs_scale=nd_s[k][:],
                start=(k == 0),
                stop=(k == 1),
            )

        def dw_out(i, engine):
            copy(engine, dw[i // 2][:, :, i % 2, :], acc["dw", i][:].rearrange("p (h f) -> p h f", h=NHEADS))

        def dw_store(h):
            nc.sync.dma_start(
                out=out_1.rearrange("h (m b) f -> m h b f", b=4)[:, :, 2 * h : 2 * h + 2, :], in_=dw[h][:]
            )

        with tc.manual_schedule():
            nc.vector.memset(warm[:], 0.0)
            nc.scalar.activation(out=warm[:], in_=warm[:], func=ACT.Exp)
            make_identity(nc, ident[:])

            load_adj0()
            load_p(0)
            load_g(0)
            load_p(1)
            load_g(1)
            load_adj1(0)
            load_adj1(1)
            load_w()
            load_x(0)
            load_x(1)

            il_adj(0, 0, "s", 3, 4)
            il_adj(0, 1, "s", 2, 4)
            il_adj(0, 0, "v", 0, 3)
            il_adj(0, 1, "v", 0, 2)
            quant(adj_c[0, 0], adj_s[0, 0], adj_grp[0, 0], E4)
            quant(adj_c[0, 1], adj_s[0, 1], adj_grp[0, 1], E4)
            exp_p(0, 0)
            exp_p(0, 1)
            mul(0, 0)
            mul(0, 1)
            exp_p(1, 0)
            exp_p(1, 1)
            quant(dz2_c[0], dz2_s[0], dz2[0], E5)
            mm_dz1(0, 0, (0, 1, 2, 3))
            mm_dz1(0, 1, (4, 5, 6, 7))
            mul(1, 0)
            mul(1, 1)
            il_adj(1, 0, "s", 1, 4)
            il_adj(1, 0, "v", 0, 1)
            quant(dz2_c[1], dz2_s[1], dz2[1], E5)
            il_adj(1, 1, "s", 1, 4)
            il_adj(1, 1, "v", 0, 1)
            quant(adj_c[1, 0], adj_s[1, 0], adj_grp[1, 0], E4)
            mm_dz1(1, 0)
            sort_w("v")
            quant(adj_c[1, 1], adj_s[1, 1], adj_grp[1, 1], E4)
            cast(0, 0, "s")
            cast(0, 1, "s")
            trans("w0", 0, w_words, (0, 1))
            mm_dz1(1, 1)
            cast(0, 2, "s")
            cast(0, 3, "s")
            il_x(0, "v", slice(64, 128))
            il_x(1, "v", slice(0, 128))
            trans("f00", 1, dz1_words(0), (0, 1))
            trans("f01", 2, dz1_words(0), (2, 3))
            trans("w1", 3, w_words, (2, 3))
            tr_out("w0", w_grp, 0, "s")
            cast(1, 3, "v")
            tr_out("f00", ft_grp[0], 0, "v")
            cast(1, 1, "s")
            cast(1, 2, "s")
            tr_out("f01", ft_grp[0], 1, "s")
            tr_out("w1", w_grp, 1, "s")
            cast(1, 0, "s")
            trans("f11", 5, dz1_words(1), (2, 3))
            trans("f10", 6, dz1_words(1), (0, 1))
            il(nd_grp[0], dz1[0], "v", slice(0, 256))
            quant(ft_c[0], ft_s[0], ft_grp[0], E5)
            quant(w_c, w_s, w_grp, E4)
            for t in range(J):
                mm_dx(0, t, (0, 1, 7, 4)[t])
            tr_out("f11", ft_grp[1], 1, "s")
            tr_out("f10", ft_grp[1], 0, "s")
            il_x(0, "v", slice(0, 64))
            il(nd_grp[1], dz1[1], "v", slice(256, 512))
            il(nd_grp[0], dz1[0], "v", slice(256, 512))
            quant(ft_c[1], ft_s[1], ft_grp[1], E5)
            dx_out(0, 0, "s")
            dx_out(0, 1, "s")
            dx_store(0, 0)
            dx_out(0, 2, "s")
            dx_out(0, 3, "s")
            dx_store(0, 1)
            for t in range(J):
                mm_dx(1, t, (2, 3, 5, 6)[t])
            quant(nd_c[0], nd_s[0], nd_grp[0], E5)
            quant(x_c[0], x_s[0], x_grp[0], E4)
            for i in range(4):
                mm_dw(0, i, (0, 1, 7, 4)[i])
            il(nd_grp[1], dz1[1], "v", slice(0, 256))
            quant(x_c[1], x_s[1], x_grp[1], E4)
            quant(nd_c[1], nd_s[1], nd_grp[1], E5)
            dx_out(1, 0, "s")
            dx_out(1, 1, "s")
            dx_store(1, 0)
            dx_out(1, 2, "s")
            dx_out(1, 3, "s")
            dx_store(1, 1)
            for i in (0, 2, 1, 3):
                mm_dw(1, i, 0)
            dw_out(0, "v")
            dw_out(2, "s")
            dw_out(1, "v")
            dw_store(0)
            dw_out(3, "s")
            dw_store(1)
